import numpy as np
import ml_dtypes


def mxq(x, axis, fmt="e4m3"):
    dtype, down = {"e4m3": (ml_dtypes.float8_e4m3fn, 7), "e5m2": (ml_dtypes.float8_e5m2, 14)}[fmt]
    v = np.moveaxis(np.asarray(x, np.float32).astype(ml_dtypes.bfloat16).astype(np.float64), axis, -1)
    blocks = v.reshape(v.shape[:-1] + (-1, 32))
    amax = np.abs(blocks).max(-1, keepdims=True)
    byte = np.maximum(np.where(amax > 0, np.frexp(amax)[1] - 1 + 127, 0) - down, 1)
    scale = np.exp2(byte - 127.0)
    codes = (blocks / scale).astype(np.float32).astype(dtype).astype(np.float64)
    return np.moveaxis((codes * scale).reshape(v.shape), -1, axis)


WIDE = False


def mx_kscale(k):
    if not WIDE:
        return np.ones(k)
    levels = np.array([10, -10, 5, -5, 0])
    a = np.random.permutation(np.resize(levels, k // 512 * 4)).reshape(k // 512, 4)
    idx = np.arange(k)
    return np.exp2(a[idx // 512, idx % 128 // 32])


BF16 = ml_dtypes.bfloat16


def bf(x):
    return np.asarray(x, np.float32).astype(BF16)


def f64(x):
    return np.asarray(x).astype(np.float64)


B, T, N, C, ORDER, KT = 2, 8, 512, 128, 4, 3
CO = C * ORDER
J = 2 * C


def sigmoid(v):
    return 1.0 / (1.0 + np.exp(-v))


def setup_inputs():
    f = mx_kscale(CO)[::ORDER]
    fr = np.tile(np.repeat(f, ORDER), KT)
    g = np.concatenate([f, np.ones(C)])
    return {"inputs": bf(np.random.standard_normal((B, T, N, C)) * f),
            "supports": bf(np.random.standard_normal((N, ORDER * N)) / np.sqrt(N)),
            "weights": bf(np.random.standard_normal((KT * CO, J)) / np.sqrt(KT * CO) / fr[:, None] * g),
            "biases": bf(np.random.standard_normal(J) * 0.3 * g)}


def reference(inputs, supports, weights, biases):
    x = f64(inputs)
    a = mxq(x, 2, "e4m3").transpose(0, 1, 3, 2) @ mxq(f64(supports), 0, "e4m3")
    z = a.reshape(B, T, C, ORDER, N).transpose(0, 1, 4, 2, 3).reshape(B, T, N, CO)
    zq = mxq(z, 3, "e4m3")
    wq = mxq(f64(weights).reshape(KT, CO, J), 1, "e4m3")
    conv = np.zeros((B, T, N, J)) + f64(biases)
    for k in range(KT):
        lag = KT - 1 - k
        conv[:, lag:] += (zq[:, :T - lag] @ wq[k])
    return (conv[..., :C] + x) * sigmoid(conv[..., C:])

@@ -1,0 +1,248 @@
+from contextlib import ExitStack
+
+import concourse.mybir as mybir
+
+BF16 = mybir.dt.bfloat16
+F32 = mybir.dt.float32
+U32 = mybir.dt.uint32
+U8 = mybir.dt.uint8
+FP8X4 = mybir.dt.float8_e4m3fn_x4
+ADD = mybir.AluOpType.add
+MULT = mybir.AluOpType.mult
+SIGMOID = mybir.ActivationFunctionType.Sigmoid
+
+B, T, N, C, ORDER, KT = 2, 8, 512, 128, 4, 3
+P = 128
+PACK = 4
+BT = B * T
+J = 2 * C
+NCH = N // P
+XG = 4
+LEAD = 2
+S_SPLIT = 384
+
+FLOPS = 2 * BT * C * ORDER * N * N + 2 * B * (1 + 2 + 3 * (T - 2)) * N * C * ORDER * J
+
+
+def by_fours(dst, src):
+    return (
+        dst.rearrange("p (c i) t -> p c t i", i=4),
+        src.rearrange("p t (c i) -> p c t i", i=4),
+    )
+
+
+def tile_conv_st_pa_t_kernel(tc, inputs, supports, weights, biases, out):
+    nc = tc.nc
+    x_dram = inputs.rearrange("b t (p j) c -> p (b t) (j c)", j=PACK)
+    s_dram = supports.rearrange("(p j) (o n) -> p o j n", j=PACK, o=ORDER)
+    w_dram = weights.rearrange("(k p t) j -> p k (t j)", k=KT, t=PACK)
+    out_dram = out.rearrange("b t (p q) c -> p (b t) (q c)", q=PACK)
+
+    with ExitStack() as ctx:
+        keep = ctx.enter_context(tc.tile_pool(name="keep", bufs=1))
+        stage = ctx.enter_context(tc.tile_pool(name="stage", bufs=2))
+        epi = ctx.enter_context(tc.tile_pool(name="epi", bufs=3))
+        psum = ctx.enter_context(tc.psum_pool(name="psum", bufs=1))
+        ctx.enter_context(tc.manual_schedule())
+
+        raw_x = keep.tile([P, BT, PACK, C], BF16, name="raw_x")
+        x_codes = keep.tile([P, BT, C], U32, name="x_codes", align_bytes=64)
+        x_scales = keep.tile([P, BT, C], U8, name="x_scales", align_bytes=64)
+        s_codes = keep.tile([P, NCH, ORDER, P], U32, name="s_codes", align_bytes=64)
+        s_scales = keep.tile([P, NCH, ORDER, P], U8, name="s_scales", align_bytes=64)
+        raw_w = keep.tile([P, KT, PACK, J], BF16, name="raw_w")
+        grp_w = keep.tile([P, KT, J, PACK], BF16, name="grp_w", align_bytes=64)
+        w_codes = keep.tile([P, KT, J], U32, name="w_codes", align_bytes=64)
+        w_scales = keep.tile([P, KT, J], U8, name="w_scales", align_bytes=64)
+        z_codes = keep.tile([P, BT, N], U32, name="z_codes", align_bytes=64)
+        z_scales = keep.tile([P, BT, N], U8, name="z_scales", align_bytes=64)
+        bias_bf = keep.tile([P, J], BF16, name="bias_bf")
+        bias_f = keep.tile([P, J], F32, name="bias_f")
+        xb = keep.tile([P, BT, PACK, C], F32, name="xb")
+        warm_in = keep.tile([P, 1], F32, name="warm_in")
+        warm_out = keep.tile([P, 1], F32, name="warm_out")
+
+        def load_x(g):
+            nc.sync.dma_start(
+                out=raw_x[:, g * XG : (g + 1) * XG].rearrange("p s j c -> p s (j c)"),
+                in_=x_dram[:, g * XG : (g + 1) * XG, :],
+            )
+
+        load_x(0)
+        raw_s = []
+        for o in range(ORDER):
+            piece = stage.tile([P, PACK, N], BF16, name="raw_s%d" % o, tag="raw_s", bufs=ORDER)
+            nc.sync.dma_start(out=piece[:], in_=s_dram[:, o])
+            raw_s.append(piece)
+        nc.sync.dma_start(out=raw_w[:].rearrange("p k t j -> p k (t j)"), in_=w_dram)
+        load_x(1)
+        nc.sync.dma_start(out=bias_bf[:], in_=biases.partition_broadcast(P))
+        load_x(2)
+        load_x(3)
+
+        nc.vector.memset(warm_in[:], 0.0)
+        nc.scalar.activation(out=warm_out[:], in_=warm_in[:], func=SIGMOID)
+
+        grp_x = {}
+
+        def regroup_x(g, on_scalar):
+            t = stage.tile([P, XG, C, PACK], BF16, name="grp_x%d" % g, tag="grp_x", align_bytes=64)
+            grp_x[g] = t
+            if on_scalar:
+                for s in range(XG):
+                    d, r = by_fours(t[:, s], raw_x[:, g * XG + s])
+                    nc.scalar.copy(out=d, in_=r)
+            else:
+                nc.vector.tensor_copy(
+                    out=t[:].rearrange("p s (c i) t -> p s c t i", i=4),
+                    in_=raw_x[:, g * XG : (g + 1) * XG].rearrange("p s t (c i) -> p s c t i", i=4),
+                )
+
+        def quantise_x(g):
+            nc.vector.quantize_mx(
+                out=x_codes[:, g * XG : (g + 1) * XG].rearrange("p s c -> p (s c)").bitcast(FP8X4),
+                scales=x_scales[:, g * XG : (g + 1) * XG].rearrange("p s c -> p (s c)"),
+                in_=grp_x[g][:].rearrange("p s c t -> p (s c t)"),
+            )
+
+        grp_s = {}
+
+        def regroup_s(o):
+            t = stage.tile([P, N, PACK], BF16, name="grp_s%d" % o, tag="grp_s", bufs=3, align_bytes=64)
+            grp_s[o] = t
+            d, r = by_fours(t[:, 0:S_SPLIT], raw_s[o][:, :, 0:S_SPLIT])
+            nc.vector.tensor_copy(out=d, in_=r)
+            d, r = by_fours(t[:, S_SPLIT:N], raw_s[o][:, :, S_SPLIT:N])
+            nc.scalar.copy(out=d, in_=r)
+
+        def quantise_s(o):
+            for ch in range(NCH):
+                nc.vector.quantize_mx(
+                    out=s_codes[:, ch, o, :].bitcast(FP8X4),
+                    scales=s_scales[:, ch, o, :],
+                    in_=grp_s[o][:, ch * P : (ch + 1) * P, :].rearrange("p w t -> p (w t)"),
+                )
+
+        def add_bias_to_x(bt):
+            nc.vector.tensor_tensor(
+                out=xb[:, bt],
+                in0=raw_x[:, bt],
+                in1=bias_f[:, 0:C].unsqueeze(1).to_broadcast([P, PACK, C]),
+                op=ADD,
+            )
+
+        z_bf = {}
+
+        def stage1(bt):
+            zt = stage.tile([P, PACK, P, ORDER], BF16, name="z_bf%d" % bt, tag="z_bf", bufs=3, align_bytes=64)
+            z_bf[bt] = zt
+            for ch in range(NCH):
+                bank = psum.tile([P, N], F32, name="s1_%d_%d" % (bt, ch), tag="s1", bufs=5)
+                nc.tensor.matmul_mx(
+                    out=bank[:],
+                    lhsT=x_codes[:, bt, :].bitcast(FP8X4),
+                    lhsT_scale=x_scales[:, bt, :],
+                    rhs=s_codes[:, ch].rearrange("p o n -> p (o n)").bitcast(FP8X4),
+                    rhs_scale=s_scales[:, ch].rearrange("p o n -> p (o n)"),
+                    start=True,
+                    stop=True,
+                )
+                nc.scalar.copy(
+                    out=zt[:, :, ch * 32 : (ch + 1) * 32, :],
+                    in_=bank[:].rearrange("p (o l q) -> p q l o", o=ORDER, q=PACK),
+                )
+
+        def quantise_z(bt):
+            nc.vector.quantize_mx(
+                out=z_codes[:, bt, :].bitcast(FP8X4),
+                scales=z_scales[:, bt, :],
+                in_=z_bf[bt][:].rearrange("p q n o -> p (q n o)"),
+            )
+
+        val = {}
+        gate = {}
+        sig = {}
+
+        def stage2(bt):
+            t = bt % T
+            taps = [(k, bt - (KT - 1 - k)) for k in range(KT) if t - (KT - 1 - k) >= 0]
+            val[bt] = epi.tile([P, PACK, C], F32, name="val%d" % bt, tag="val")
+            gate[bt] = epi.tile([P, PACK, C], F32, name="gate%d" % bt, tag="gate")
+            for h in range(2):
+                bank = psum.tile([P, 2, J], F32, name="s2_%d_%d" % (bt, h), tag="s2", bufs=3)
+                for qq in range(2):
+                    q = 2 * h + qq
+                    for n_done, (k, src) in enumerate(taps):
+                        nc.tensor.matmul_mx(
+                            out=bank[:, qq, :],
+                            lhsT=z_codes[:, src, q * P : (q + 1) * P].bitcast(FP8X4),
+                            lhsT_scale=z_scales[:, src, q * P : (q + 1) * P],
+                            rhs=w_codes[:, k, :].bitcast(FP8X4),
+                            rhs_scale=w_scales[:, k, :],
+                            start=(n_done == 0),
+                            stop=(n_done == len(taps) - 1),
+                        )
+                nc.vector.tensor_tensor(
+                    out=gate[bt][:, 2 * h : 2 * h + 2, :],
+                    in0=bank[:, :, C:J],
+                    in1=bias_f[:, C:J].unsqueeze(1).to_broadcast([P, 2, C]),
+                    op=ADD,
+                )
+                nc.vector.tensor_tensor(
+                    out=val[bt][:, 2 * h : 2 * h + 2, :],
+                    in0=bank[:, :, 0:C],
+                    in1=xb[:, bt, 2 * h : 2 * h + 2, :],
+                    op=ADD,
+                )
+            sig[bt] = epi.tile([P, PACK, C], F32, name="sig%d" % bt, tag="sig")
+            nc.scalar.activation(out=sig[bt][:], in_=gate[bt][:], func=SIGMOID)
+
+        def finish(bt):
+            res = epi.tile([P, PACK, C], F32, name="res%d" % bt, tag="res")
+            nc.vector.tensor_tensor(out=res[:], in0=val[bt][:], in1=sig[bt][:], op=MULT)
+            nc.sync.dma_start(out=out_dram[:, bt, :], in_=res[:].rearrange("p q c -> p (q c)"))
+
+        regroup_x(0, True)
+        regroup_s(0)
+        quantise_x(0)
+        regroup_s(1)
+        quantise_s(0)
+        regroup_s(2)
+        quantise_s(1)
+        regroup_s(3)
+        quantise_s(2)
+        for k in range(KT):
+            d, r = by_fours(grp_w[:, k], raw_w[:, k])
+            nc.vector.tensor_copy(out=d, in_=r)
+        quantise_s(3)
+        stage1(0)
+        regroup_x(1, False)
+        for k in range(KT):
+            nc.vector.quantize_mx(
+                out=w_codes[:, k, :].bitcast(FP8X4),
+                scales=w_scales[:, k, :],
+                in_=grp_w[:, k].rearrange("p j t -> p (j t)"),
+            )
+        stage1(1)
+        nc.vector.tensor_copy(out=bias_f[:], in_=bias_bf[:])
+        add_bias_to_x(0)
+        quantise_x(1)
+        quantise_z(0)
+
+        regroup_at = {1: 2, 5: 3}
+        quantise_at = {2: 2, 6: 3}
+        for s in range(BT + 1):
+            if s + LEAD < BT:
+                stage1(s + LEAD)
+            if s + 1 < BT:
+                quantise_z(s + 1)
+            if s >= 1:
+                finish(s - 1)
+            if s < BT:
+                stage2(s)
+            if s + 1 < BT:
+                add_bias_to_x(s + 1)
+            if s in regroup_at:
+                regroup_x(regroup_at[s], False)
+            if s in quantise_at:
+                quantise_x(quantise_at[s])

@@ -1,6 +1,7 @@
 from contextlib import ExitStack
 
 import concourse.mybir as mybir
+from concourse.masks import make_identity
 
 BF16 = mybir.dt.bfloat16
 F32 = mybir.dt.float32
@@ -19,7 +20,9 @@ J = 2 * C
 NCH = N // P
 XG = 4
 LEAD = 2
-S_SPLIT = 384
+S_SPLIT = 352
+XB_ON_PE = 4
+XB_HEAD = 4
 
 FLOPS = 2 * BT * C * ORDER * N * N + 2 * B * (1 + 2 + 3 * (T - 2)) * N * C * ORDER * J
 
@@ -43,7 +46,6 @@ def tile_conv_st_pa_t_kernel(tc, inputs, supports, weights, biases, out):
         stage = ctx.enter_context(tc.tile_pool(name="stage", bufs=2))
         epi = ctx.enter_context(tc.tile_pool(name="epi", bufs=3))
         psum = ctx.enter_context(tc.psum_pool(name="psum", bufs=1))
-        ctx.enter_context(tc.manual_schedule())
 
         raw_x = keep.tile([P, BT, PACK, C], BF16, name="raw_x")
         x_codes = keep.tile([P, BT, C], U32, name="x_codes", align_bytes=64)
@@ -56,7 +58,9 @@ def tile_conv_st_pa_t_kernel(tc, inputs, supports, weights, biases, out):
         w_scales = keep.tile([P, KT, J], U8, name="w_scales", align_bytes=64)
         z_codes = keep.tile([P, BT, N], U32, name="z_codes", align_bytes=64)
         z_scales = keep.tile([P, BT, N], U8, name="z_scales", align_bytes=64)
-        bias_bf = keep.tile([P, J], BF16, name="bias_bf")
+        bias_row = keep.tile([P, PACK + 1, C], BF16, name="bias_row")
+        ident = keep.tile([P, P], BF16, name="ident")
+        ones = keep.tile([P, P], BF16, name="ones")
         bias_f = keep.tile([P, J], F32, name="bias_f")
         xb = keep.tile([P, BT, PACK, C], F32, name="xb")
         warm_in = keep.tile([P, 1], F32, name="warm_in")
@@ -68,6 +72,15 @@ def tile_conv_st_pa_t_kernel(tc, inputs, supports, weights, biases, out):
                 in_=x_dram[:, g * XG : (g + 1) * XG, :],
             )
 
+        nc.vector.memset(warm_in[:], 0.0)
+        nc.vector.memset(bias_row[:], 0.0)
+        nc.vector.memset(ones[:], 1.0)
+        make_identity(nc, ident[:])
+        nc.sync.dma_start(
+            out=bias_row[0:1, 0:PACK, :],
+            in_=biases[0:C].unsqueeze(0).unsqueeze(0).to_broadcast([1, PACK, C]),
+        )
+        nc.sync.dma_start(out=bias_row[0:1, PACK, :], in_=biases[C:J].unsqueeze(0))
         load_x(0)
         raw_s = []
         for o in range(ORDER):
@@ -76,11 +89,9 @@ def tile_conv_st_pa_t_kernel(tc, inputs, supports, weights, biases, out):
             raw_s.append(piece)
         nc.sync.dma_start(out=raw_w[:].rearrange("p k t j -> p k (t j)"), in_=w_dram)
         load_x(1)
-        nc.sync.dma_start(out=bias_bf[:], in_=biases.partition_broadcast(P))
         load_x(2)
         load_x(3)
 
-        nc.vector.memset(warm_in[:], 0.0)
         nc.scalar.activation(out=warm_out[:], in_=warm_in[:], func=SIGMOID)
 
         grp_x = {}
@@ -124,6 +135,18 @@ def tile_conv_st_pa_t_kernel(tc, inputs, supports, weights, biases, out):
                 )
 
         def add_bias_to_x(bt):
+            if bt < XB_ON_PE:
+                bank = psum.tile([P, N], F32, name="xb_%d" % bt, tag="s1", bufs=5)
+                nc.tensor.matmul(
+                    out=bank[:], lhsT=ident[:], rhs=raw_x[:, bt].rearrange("p j c -> p (j c)"),
+                    start=True, stop=False,
+                )
+                nc.tensor.matmul(
+                    out=bank[:], lhsT=ones[:], rhs=bias_row[:, 0:PACK].rearrange("p r c -> p (r c)"),
+                    start=False, stop=True,
+                )
+                nc.scalar.copy(out=xb[:, bt].rearrange("p j c -> p (j c)"), in_=bank[:])
+                return
             nc.vector.tensor_tensor(
                 out=xb[:, bt],
                 in0=raw_x[:, bt],
@@ -168,6 +191,7 @@ def tile_conv_st_pa_t_kernel(tc, inputs, supports, weights, biases, out):
             taps = [(k, bt - (KT - 1 - k)) for k in range(KT) if t - (KT - 1 - k) >= 0]
             val[bt] = epi.tile([P, PACK, C], F32, name="val%d" % bt, tag="val")
             gate[bt] = epi.tile([P, PACK, C], F32, name="gate%d" % bt, tag="gate")
+            sig[bt] = epi.tile([P, PACK, C], F32, name="sig%d" % bt, tag="sig")
             for h in range(2):
                 bank = psum.tile([P, 2, J], F32, name="s2_%d_%d" % (bt, h), tag="s2", bufs=3)
                 for qq in range(2):
@@ -194,15 +218,32 @@ def tile_conv_st_pa_t_kernel(tc, inputs, supports, weights, biases, out):
                     in1=xb[:, bt, 2 * h : 2 * h + 2, :],
                     op=ADD,
                 )
-            sig[bt] = epi.tile([P, PACK, C], F32, name="sig%d" % bt, tag="sig")
-            nc.scalar.activation(out=sig[bt][:], in_=gate[bt][:], func=SIGMOID)
+                if bt == BT - 1:
+                    nc.scalar.activation(
+                        out=sig[bt][:, 2 * h : 2 * h + 2, :], in_=gate[bt][:, 2 * h : 2 * h + 2, :], func=SIGMOID
+                    )
+            if bt < BT - 1:
+                nc.scalar.activation(out=sig[bt][:], in_=gate[bt][:], func=SIGMOID)
 
         def finish(bt):
             res = epi.tile([P, PACK, C], F32, name="res%d" % bt, tag="res")
-            nc.vector.tensor_tensor(out=res[:], in0=val[bt][:], in1=sig[bt][:], op=MULT)
-            nc.sync.dma_start(out=out_dram[:, bt, :], in_=res[:].rearrange("p q c -> p (q c)"))
+            cuts = [(0, PACK)] if bt < BT - 1 else [(0, 2), (2, PACK)]
+            for lo, hi in cuts:
+                eng = nc.gpsimd if bt < BT - 1 else nc.vector
+                eng.tensor_tensor(out=res[:, lo:hi], in0=val[bt][:, lo:hi], in1=sig[bt][:, lo:hi], op=MULT)
+                nc.sync.dma_start(
+                    out=out_dram[:, bt, lo * C : hi * C], in_=res[:, lo:hi].rearrange("p q c -> p (q c)")
+                )
 
-        regroup_x(0, True)
+        regroup_x(0, False)
+        bank = psum.tile([P, 2, J], F32, name="bias_bank", tag="s2", bufs=3)
+        nc.tensor.matmul(
+            out=bank[:, 0, :], lhsT=ones[:], rhs=bias_row[:, PACK - 1 : PACK + 1].rearrange("p r c -> p (r c)"),
+            start=True, stop=True,
+        )
+        nc.scalar.copy(out=bias_f[:], in_=bank[:, 0, :])
+        for bt in range(XB_HEAD):
+            add_bias_to_x(bt)
         regroup_s(0)
         quantise_x(0)
         regroup_s(1)
@@ -211,11 +252,12 @@ def tile_conv_st_pa_t_kernel(tc, inputs, supports, weights, biases, out):
         quantise_s(1)
         regroup_s(3)
         quantise_s(2)
+        quantise_s(3)
+        stage1(0)
+        stage1(1)
         for k in range(KT):
             d, r = by_fours(grp_w[:, k], raw_w[:, k])
             nc.vector.tensor_copy(out=d, in_=r)
-        quantise_s(3)
-        stage1(0)
         regroup_x(1, False)
         for k in range(KT):
             nc.vector.quantize_mx(
@@ -223,9 +265,6 @@ def tile_conv_st_pa_t_kernel(tc, inputs, supports, weights, biases, out):
                 scales=w_scales[:, k, :],
                 in_=grp_w[:, k].rearrange("p j t -> p (j t)"),
             )
-        stage1(1)
-        nc.vector.tensor_copy(out=bias_f[:], in_=bias_bf[:])
-        add_bias_to_x(0)
         quantise_x(1)
         quantise_z(0)
 
@@ -240,8 +279,8 @@ def tile_conv_st_pa_t_kernel(tc, inputs, supports, weights, biases, out):
                 finish(s - 1)
             if s < BT:
                 stage2(s)
-            if s + 1 < BT:
-                add_bias_to_x(s + 1)
+            if XB_HEAD <= s + 2 < BT:
+                add_bias_to_x(s + 2)
             if s in regroup_at:
                 regroup_x(regroup_at[s], False)
             if s in quantise_at:

@@ -18,11 +18,15 @@ PACK = 4
 BT = B * T
 J = 2 * C
 NCH = N // P
-XG = 4
 LEAD = 2
-S_SPLIT = 352
-XB_ON_PE = 4
-XB_HEAD = 4
+X_GROUPS = [(0, 4), (4, 8), (8, 12), (12, 16)]
+S_SPLITS = [352, 352, 352, 352]
+XB_PE = (0, 1, 2, 3)
+XB_G = (4, 5, 6, 7, 8, 9, 10, 11, 12, 13, 14, 15)
+EVAC_V = ((1, 3), (3, 3), (5, 3), (7, 3), (9, 3), (11, 3), (13, 3), (15, 3))
+RG_AT = {1: 2, 5: 3}
+Q_AT = {2: 2, 6: 3}
+FINE = {15: 1}
 
 FLOPS = 2 * BT * C * ORDER * N * N + 2 * B * (1 + 2 + 3 * (T - 2)) * N * C * ORDER * J
 
@@ -44,7 +48,7 @@ def tile_conv_st_pa_t_kernel(tc, inputs, supports, weights, biases, out):
     with ExitStack() as ctx:
         keep = ctx.enter_context(tc.tile_pool(name="keep", bufs=1))
         stage = ctx.enter_context(tc.tile_pool(name="stage", bufs=2))
-        epi = ctx.enter_context(tc.tile_pool(name="epi", bufs=3))
+        epi = ctx.enter_context(tc.tile_pool(name="epi", bufs=6))
         psum = ctx.enter_context(tc.psum_pool(name="psum", bufs=1))
 
         raw_x = keep.tile([P, BT, PACK, C], BF16, name="raw_x")
@@ -67,10 +71,19 @@ def tile_conv_st_pa_t_kernel(tc, inputs, supports, weights, biases, out):
         warm_out = keep.tile([P, 1], F32, name="warm_out")
 
         def load_x(g):
+            lo, hi = X_GROUPS[g]
             nc.sync.dma_start(
-                out=raw_x[:, g * XG : (g + 1) * XG].rearrange("p s j c -> p s (j c)"),
-                in_=x_dram[:, g * XG : (g + 1) * XG, :],
+                out=raw_x[:, lo:hi].rearrange("p s j c -> p s (j c)"), in_=x_dram[:, lo:hi, :]
             )
+
+        raw_s = {}
+
+        def load_s(o):
+            raw_s[o] = stage.tile([P, PACK, N], BF16, name="raw_s%d" % o, tag="raw_s", bufs=ORDER)
+            nc.sync.dma_start(out=raw_s[o][:], in_=s_dram[:, o])
+
+        def load_w(k):
+            nc.sync.dma_start(out=raw_w[:, k].rearrange("p t j -> p (t j)"), in_=w_dram[:, k, :])
 
         nc.vector.memset(warm_in[:], 0.0)
         nc.vector.memset(bias_row[:], 0.0)
@@ -82,48 +95,44 @@ def tile_conv_st_pa_t_kernel(tc, inputs, supports, weights, biases, out):
         )
         nc.sync.dma_start(out=bias_row[0:1, PACK, :], in_=biases[C:J].unsqueeze(0))
         load_x(0)
-        raw_s = []
-        for o in range(ORDER):
-            piece = stage.tile([P, PACK, N], BF16, name="raw_s%d" % o, tag="raw_s", bufs=ORDER)
-            nc.sync.dma_start(out=piece[:], in_=s_dram[:, o])
-            raw_s.append(piece)
-        nc.sync.dma_start(out=raw_w[:].rearrange("p k t j -> p k (t j)"), in_=w_dram)
+        load_s(0)
+        load_s(1)
+        load_s(2)
+        load_s(3)
+        load_w(2)
+        load_w(1)
+        load_w(0)
         load_x(1)
         load_x(2)
         load_x(3)
-
         nc.scalar.activation(out=warm_out[:], in_=warm_in[:], func=SIGMOID)
 
         grp_x = {}
 
-        def regroup_x(g, on_scalar):
-            t = stage.tile([P, XG, C, PACK], BF16, name="grp_x%d" % g, tag="grp_x", align_bytes=64)
-            grp_x[g] = t
-            if on_scalar:
-                for s in range(XG):
-                    d, r = by_fours(t[:, s], raw_x[:, g * XG + s])
-                    nc.scalar.copy(out=d, in_=r)
-            else:
-                nc.vector.tensor_copy(
-                    out=t[:].rearrange("p s (c i) t -> p s c t i", i=4),
-                    in_=raw_x[:, g * XG : (g + 1) * XG].rearrange("p s t (c i) -> p s c t i", i=4),
-                )
+        def regroup_x(g):
+            lo, hi = X_GROUPS[g]
+            grp_x[g] = stage.tile([P, hi - lo, C, PACK], BF16, name="grp_x%d" % g, tag="grp_x", align_bytes=64)
+            nc.vector.tensor_copy(
+                out=grp_x[g][:].rearrange("p s (c i) t -> p s c t i", i=4),
+                in_=raw_x[:, lo:hi].rearrange("p s t (c i) -> p s c t i", i=4),
+            )
 
         def quantise_x(g):
+            lo, hi = X_GROUPS[g]
             nc.vector.quantize_mx(
-                out=x_codes[:, g * XG : (g + 1) * XG].rearrange("p s c -> p (s c)").bitcast(FP8X4),
-                scales=x_scales[:, g * XG : (g + 1) * XG].rearrange("p s c -> p (s c)"),
+                out=x_codes[:, lo:hi].rearrange("p s c -> p (s c)").bitcast(FP8X4),
+                scales=x_scales[:, lo:hi].rearrange("p s c -> p (s c)"),
                 in_=grp_x[g][:].rearrange("p s c t -> p (s c t)"),
             )
 
         grp_s = {}
 
         def regroup_s(o):
-            t = stage.tile([P, N, PACK], BF16, name="grp_s%d" % o, tag="grp_s", bufs=3, align_bytes=64)
-            grp_s[o] = t
-            d, r = by_fours(t[:, 0:S_SPLIT], raw_s[o][:, :, 0:S_SPLIT])
+            cut = S_SPLITS[o]
+            grp_s[o] = stage.tile([P, N, PACK], BF16, name="grp_s%d" % o, tag="grp_s", bufs=3, align_bytes=64)
+            d, r = by_fours(grp_s[o][:, 0:cut], raw_s[o][:, :, 0:cut])
             nc.vector.tensor_copy(out=d, in_=r)
-            d, r = by_fours(t[:, S_SPLIT:N], raw_s[o][:, :, S_SPLIT:N])
+            d, r = by_fours(grp_s[o][:, cut:N], raw_s[o][:, :, cut:N])
             nc.scalar.copy(out=d, in_=r)
 
         def quantise_s(o):
@@ -134,8 +143,19 @@ def tile_conv_st_pa_t_kernel(tc, inputs, supports, weights, biases, out):
                     in_=grp_s[o][:, ch * P : (ch + 1) * P, :].rearrange("p w t -> p (w t)"),
                 )
 
+        def regroup_w(k):
+            d, r = by_fours(grp_w[:, k], raw_w[:, k])
+            nc.vector.tensor_copy(out=d, in_=r)
+
+        def quantise_w(k):
+            nc.vector.quantize_mx(
+                out=w_codes[:, k, :].bitcast(FP8X4),
+                scales=w_scales[:, k, :],
+                in_=grp_w[:, k].rearrange("p j t -> p (j t)"),
+            )
+
         def add_bias_to_x(bt):
-            if bt < XB_ON_PE:
+            if bt in XB_PE:
                 bank = psum.tile([P, N], F32, name="xb_%d" % bt, tag="s1", bufs=5)
                 nc.tensor.matmul(
                     out=bank[:], lhsT=ident[:], rhs=raw_x[:, bt].rearrange("p j c -> p (j c)"),
@@ -146,18 +166,19 @@ def tile_conv_st_pa_t_kernel(tc, inputs, supports, weights, biases, out):
                     start=False, stop=True,
                 )
                 nc.scalar.copy(out=xb[:, bt].rearrange("p j c -> p (j c)"), in_=bank[:])
-                return
-            nc.vector.tensor_tensor(
-                out=xb[:, bt],
-                in0=raw_x[:, bt],
-                in1=bias_f[:, 0:C].unsqueeze(1).to_broadcast([P, PACK, C]),
-                op=ADD,
-            )
+            else:
+                eng = nc.gpsimd if bt in XB_G else nc.vector
+                eng.tensor_tensor(
+                    out=xb[:, bt],
+                    in0=raw_x[:, bt],
+                    in1=bias_f[:, 0:C].unsqueeze(1).to_broadcast([P, PACK, C]),
+                    op=ADD,
+                )
 
         z_bf = {}
 
         def stage1(bt):
-            zt = stage.tile([P, PACK, P, ORDER], BF16, name="z_bf%d" % bt, tag="z_bf", bufs=3, align_bytes=64)
+            zt = stage.tile([P, PACK, P, ORDER], BF16, name="z_bf%d" % bt, tag="z_bf", bufs=4, align_bytes=64)
             z_bf[bt] = zt
             for ch in range(NCH):
                 bank = psum.tile([P, N], F32, name="s1_%d_%d" % (bt, ch), tag="s1", bufs=5)
@@ -170,10 +191,12 @@ def tile_conv_st_pa_t_kernel(tc, inputs, supports, weights, biases, out):
                     start=True,
                     stop=True,
                 )
-                nc.scalar.copy(
-                    out=zt[:, :, ch * 32 : (ch + 1) * 32, :],
-                    in_=bank[:].rearrange("p (o l q) -> p q l o", o=ORDER, q=PACK),
-                )
+                dst = zt[:, :, ch * 32 : (ch + 1) * 32, :]
+                src = bank[:].rearrange("p (o l q) -> p q l o", o=ORDER, q=PACK)
+                if (bt, ch) in EVAC_V:
+                    nc.vector.tensor_copy(out=dst, in_=src)
+                else:
+                    nc.scalar.copy(out=dst, in_=src)
 
         def quantise_z(bt):
             nc.vector.quantize_mx(
@@ -192,6 +215,7 @@ def tile_conv_st_pa_t_kernel(tc, inputs, supports, weights, biases, out):
             val[bt] = epi.tile([P, PACK, C], F32, name="val%d" % bt, tag="val")
             gate[bt] = epi.tile([P, PACK, C], F32, name="gate%d" % bt, tag="gate")
             sig[bt] = epi.tile([P, PACK, C], F32, name="sig%d" % bt, tag="sig")
+            width = FINE.get(bt, PACK)
             for h in range(2):
                 bank = psum.tile([P, 2, J], F32, name="s2_%d_%d" % (bt, h), tag="s2", bufs=3)
                 for qq in range(2):
@@ -206,44 +230,53 @@ def tile_conv_st_pa_t_kernel(tc, inputs, supports, weights, biases, out):
                             start=(n_done == 0),
                             stop=(n_done == len(taps) - 1),
                         )
-                nc.vector.tensor_tensor(
-                    out=gate[bt][:, 2 * h : 2 * h + 2, :],
-                    in0=bank[:, :, C:J],
-                    in1=bias_f[:, C:J].unsqueeze(1).to_broadcast([P, 2, C]),
-                    op=ADD,
-                )
-                nc.vector.tensor_tensor(
-                    out=val[bt][:, 2 * h : 2 * h + 2, :],
-                    in0=bank[:, :, 0:C],
-                    in1=xb[:, bt, 2 * h : 2 * h + 2, :],
-                    op=ADD,
-                )
-                if bt == BT - 1:
-                    nc.scalar.activation(
-                        out=sig[bt][:, 2 * h : 2 * h + 2, :], in_=gate[bt][:, 2 * h : 2 * h + 2, :], func=SIGMOID
+                step = min(width, 2)
+                for a in range(0, 2, step):
+                    lo = 2 * h + a
+                    nc.vector.tensor_tensor(
+                        out=gate[bt][:, lo : lo + step, :],
+                        in0=bank[:, a : a + step, C:J],
+                        in1=bias_f[:, C:J].unsqueeze(1).to_broadcast([P, step, C]),
+                        op=ADD,
                     )
-            if bt < BT - 1:
+                    if width <= 2:
+                        nc.scalar.activation(
+                            out=sig[bt][:, lo : lo + step, :], in_=gate[bt][:, lo : lo + step, :], func=SIGMOID
+                        )
+                    nc.vector.tensor_tensor(
+                        out=val[bt][:, lo : lo + step, :],
+                        in0=bank[:, a : a + step, 0:C],
+                        in1=xb[:, bt, lo : lo + step, :],
+                        op=ADD,
+                    )
+            if width > 2:
                 nc.scalar.activation(out=sig[bt][:], in_=gate[bt][:], func=SIGMOID)
 
         def finish(bt):
             res = epi.tile([P, PACK, C], F32, name="res%d" % bt, tag="res")
-            cuts = [(0, PACK)] if bt < BT - 1 else [(0, 2), (2, PACK)]
-            for lo, hi in cuts:
-                eng = nc.gpsimd if bt < BT - 1 else nc.vector
+            width = FINE.get(bt, PACK)
+            eng = nc.gpsimd if bt not in FINE else nc.vector
+            for lo in range(0, PACK, width):
+                hi = lo + width
                 eng.tensor_tensor(out=res[:, lo:hi], in0=val[bt][:, lo:hi], in1=sig[bt][:, lo:hi], op=MULT)
                 nc.sync.dma_start(
                     out=out_dram[:, bt, lo * C : hi * C], in_=res[:, lo:hi].rearrange("p q c -> p (q c)")
                 )
 
-        regroup_x(0, False)
-        bank = psum.tile([P, 2, J], F32, name="bias_bank", tag="s2", bufs=3)
-        nc.tensor.matmul(
-            out=bank[:, 0, :], lhsT=ones[:], rhs=bias_row[:, PACK - 1 : PACK + 1].rearrange("p r c -> p (r c)"),
-            start=True, stop=True,
-        )
-        nc.scalar.copy(out=bias_f[:], in_=bank[:, 0, :])
-        for bt in range(XB_HEAD):
-            add_bias_to_x(bt)
+        def spread_bias():
+            bank = psum.tile([P, 2, J], F32, name="bias_bank", tag="s2", bufs=3)
+            nc.tensor.matmul(
+                out=bank[:, 0, :], lhsT=ones[:], rhs=bias_row[:, PACK - 1 : PACK + 1].rearrange("p r c -> p (r c)"),
+                start=True, stop=True,
+            )
+            nc.scalar.copy(out=bias_f[:], in_=bank[:, 0, :])
+
+        regroup_x(0)
+        spread_bias()
+        add_bias_to_x(0)
+        add_bias_to_x(1)
+        add_bias_to_x(2)
+        add_bias_to_x(3)
         regroup_s(0)
         quantise_x(0)
         regroup_s(1)
@@ -255,21 +288,15 @@ def tile_conv_st_pa_t_kernel(tc, inputs, supports, weights, biases, out):
         quantise_s(3)
         stage1(0)
         stage1(1)
-        for k in range(KT):
-            d, r = by_fours(grp_w[:, k], raw_w[:, k])
-            nc.vector.tensor_copy(out=d, in_=r)
-        regroup_x(1, False)
-        for k in range(KT):
-            nc.vector.quantize_mx(
-                out=w_codes[:, k, :].bitcast(FP8X4),
-                scales=w_scales[:, k, :],
-                in_=grp_w[:, k].rearrange("p j t -> p (j t)"),
-            )
+        regroup_w(0)
+        regroup_w(1)
+        regroup_w(2)
+        regroup_x(1)
+        quantise_w(0)
+        quantise_w(1)
+        quantise_w(2)
         quantise_x(1)
         quantise_z(0)
-
-        regroup_at = {1: 2, 5: 3}
-        quantise_at = {2: 2, 6: 3}
         for s in range(BT + 1):
             if s + LEAD < BT:
                 stage1(s + LEAD)
@@ -279,9 +306,9 @@ def tile_conv_st_pa_t_kernel(tc, inputs, supports, weights, biases, out):
                 finish(s - 1)
             if s < BT:
                 stage2(s)
-            if XB_HEAD <= s + 2 < BT:
+            if 4 <= s + 2 < BT:
                 add_bias_to_x(s + 2)
-            if s in regroup_at:
-                regroup_x(regroup_at[s], False)
-            if s in quantise_at:
-                quantise_x(quantise_at[s])
+            if s in RG_AT:
+                regroup_x(RG_AT[s])
+            if s in Q_AT:
+                quantise_x(Q_AT[s])

@@ -19,13 +19,13 @@ BT = B * T
 J = 2 * C
 NCH = N // P
 LEAD = 2
-X_GROUPS = [(0, 4), (4, 8), (8, 12), (12, 16)]
-S_SPLITS = [352, 352, 352, 352]
+X_GROUPS = [(0, 2), (2, 4), (4, 8), (8, 12), (12, 16)]
+S_SPLITS = [288, 288, 288, 320]
 XB_PE = (0, 1, 2, 3)
-XB_G = (4, 5, 6, 7, 8, 9, 10, 11, 12, 13, 14, 15)
-EVAC_V = ((1, 3), (3, 3), (5, 3), (7, 3), (9, 3), (11, 3), (13, 3), (15, 3))
-RG_AT = {1: 2, 5: 3}
-Q_AT = {2: 2, 6: 3}
+XB_G = ()
+EVAC_V = ((5, 3), (11, 3))
+RG_AT = {0: 2, 3: 3, 7: 4}
+Q_AT = {1: 2, 4: 3, 8: 4}
 FINE = {15: 1}
 
 FLOPS = 2 * BT * C * ORDER * N * N + 2 * B * (1 + 2 + 3 * (T - 2)) * N * C * ORDER * J
@@ -48,7 +48,7 @@ def tile_conv_st_pa_t_kernel(tc, inputs, supports, weights, biases, out):
     with ExitStack() as ctx:
         keep = ctx.enter_context(tc.tile_pool(name="keep", bufs=1))
         stage = ctx.enter_context(tc.tile_pool(name="stage", bufs=2))
-        epi = ctx.enter_context(tc.tile_pool(name="epi", bufs=6))
+        epi = ctx.enter_context(tc.tile_pool(name="epi", bufs=4))
         psum = ctx.enter_context(tc.psum_pool(name="psum", bufs=1))
 
         raw_x = keep.tile([P, BT, PACK, C], BF16, name="raw_x")
@@ -94,17 +94,18 @@ def tile_conv_st_pa_t_kernel(tc, inputs, supports, weights, biases, out):
             in_=biases[0:C].unsqueeze(0).unsqueeze(0).to_broadcast([1, PACK, C]),
         )
         nc.sync.dma_start(out=bias_row[0:1, PACK, :], in_=biases[C:J].unsqueeze(0))
-        load_x(0)
         load_s(0)
+        load_x(0)
         load_s(1)
         load_s(2)
         load_s(3)
+        load_x(1)
         load_w(2)
         load_w(1)
         load_w(0)
-        load_x(1)
         load_x(2)
         load_x(3)
+        load_x(4)
         nc.scalar.activation(out=warm_out[:], in_=warm_in[:], func=SIGMOID)
 
         grp_x = {}
@@ -112,10 +113,15 @@ def tile_conv_st_pa_t_kernel(tc, inputs, supports, weights, biases, out):
         def regroup_x(g):
             lo, hi = X_GROUPS[g]
             grp_x[g] = stage.tile([P, hi - lo, C, PACK], BF16, name="grp_x%d" % g, tag="grp_x", align_bytes=64)
-            nc.vector.tensor_copy(
-                out=grp_x[g][:].rearrange("p s (c i) t -> p s c t i", i=4),
-                in_=raw_x[:, lo:hi].rearrange("p s t (c i) -> p s c t i", i=4),
-            )
+            if g in (0,):
+                for s in range(hi - lo):
+                    d, r = by_fours(grp_x[g][:, s], raw_x[:, lo + s])
+                    nc.scalar.copy(out=d, in_=r)
+            else:
+                nc.vector.tensor_copy(
+                    out=grp_x[g][:].rearrange("p s (c i) t -> p s c t i", i=4),
+                    in_=raw_x[:, lo:hi].rearrange("p s t (c i) -> p s c t i", i=4),
+                )
 
         def quantise_x(g):
             lo, hi = X_GROUPS[g]
@@ -135,8 +141,8 @@ def tile_conv_st_pa_t_kernel(tc, inputs, supports, weights, biases, out):
             d, r = by_fours(grp_s[o][:, cut:N], raw_s[o][:, :, cut:N])
             nc.scalar.copy(out=d, in_=r)
 
-        def quantise_s(o):
-            for ch in range(NCH):
+        def quantise_s(o, chunks=(0, 1, 2, 3)):
+            for ch in chunks:
                 nc.vector.quantize_mx(
                     out=s_codes[:, ch, o, :].bitcast(FP8X4),
                     scales=s_scales[:, ch, o, :],
@@ -178,7 +184,7 @@ def tile_conv_st_pa_t_kernel(tc, inputs, supports, weights, biases, out):
         z_bf = {}
 
         def stage1(bt):
-            zt = stage.tile([P, PACK, P, ORDER], BF16, name="z_bf%d" % bt, tag="z_bf", bufs=4, align_bytes=64)
+            zt = stage.tile([P, PACK, P, ORDER], BF16, name="z_bf%d" % bt, tag="z_bf", bufs=3, align_bytes=64)
             z_bf[bt] = zt
             for ch in range(NCH):
                 bank = psum.tile([P, N], F32, name="s1_%d_%d" % (bt, ch), tag="s1", bufs=5)
@@ -271,32 +277,33 @@ def tile_conv_st_pa_t_kernel(tc, inputs, supports, weights, biases, out):
             )
             nc.scalar.copy(out=bias_f[:], in_=bank[:, 0, :])
 
+        regroup_s(0)
         regroup_x(0)
+        regroup_s(1)
+        quantise_s(0)
+        quantise_x(0)
+        regroup_s(2)
+        quantise_s(1)
         spread_bias()
         add_bias_to_x(0)
         add_bias_to_x(1)
-        add_bias_to_x(2)
-        add_bias_to_x(3)
-        regroup_s(0)
-        quantise_x(0)
-        regroup_s(1)
-        quantise_s(0)
-        regroup_s(2)
-        quantise_s(1)
         regroup_s(3)
-        quantise_s(2)
-        quantise_s(3)
+        for ch in range(NCH):
+            quantise_s(2, (ch,))
+            quantise_s(3, (ch,))
         stage1(0)
         stage1(1)
-        regroup_w(0)
-        regroup_w(1)
-        regroup_w(2)
         regroup_x(1)
-        quantise_w(0)
-        quantise_w(1)
-        quantise_w(2)
+        regroup_w(2)
         quantise_x(1)
+        quantise_w(2)
         quantise_z(0)
+        add_bias_to_x(2)
+        add_bias_to_x(3)
+        regroup_w(1)
+        regroup_w(0)
+        quantise_w(1)
+        quantise_w(0)
         for s in range(BT + 1):
             if s + LEAD < BT:
                 stage1(s + LEAD)

@@ -21,12 +21,12 @@ NCH = N // P
 LEAD = 2
 X_GROUPS = [(0, 2), (2, 4), (4, 8), (8, 12), (12, 16)]
 S_SPLITS = [288, 288, 288, 320]
-XB_PE = (0, 1, 2, 3)
+XB_PE = (0, 1)
 XB_G = ()
-EVAC_V = ((5, 3), (11, 3))
+EVAC_V = ()
 RG_AT = {0: 2, 3: 3, 7: 4}
 Q_AT = {1: 2, 4: 3, 8: 4}
-FINE = {15: 1}
+FINE = {15: 2}
 
 FLOPS = 2 * BT * C * ORDER * N * N + 2 * B * (1 + 2 + 3 * (T - 2)) * N * C * ORDER * J
 
@@ -48,8 +48,9 @@ def tile_conv_st_pa_t_kernel(tc, inputs, supports, weights, biases, out):
     with ExitStack() as ctx:
         keep = ctx.enter_context(tc.tile_pool(name="keep", bufs=1))
         stage = ctx.enter_context(tc.tile_pool(name="stage", bufs=2))
-        epi = ctx.enter_context(tc.tile_pool(name="epi", bufs=4))
+        epi = ctx.enter_context(tc.tile_pool(name="epi", bufs=3))
         psum = ctx.enter_context(tc.psum_pool(name="psum", bufs=1))
+        ctx.enter_context(tc.manual_schedule())
 
         raw_x = keep.tile([P, BT, PACK, C], BF16, name="raw_x")
         x_codes = keep.tile([P, BT, C], U32, name="x_codes", align_bytes=64)
@@ -89,19 +90,23 @@ def tile_conv_st_pa_t_kernel(tc, inputs, supports, weights, biases, out):
         nc.vector.memset(bias_row[:], 0.0)
         nc.vector.memset(ones[:], 1.0)
         make_identity(nc, ident[:])
-        nc.sync.dma_start(
-            out=bias_row[0:1, 0:PACK, :],
-            in_=biases[0:C].unsqueeze(0).unsqueeze(0).to_broadcast([1, PACK, C]),
-        )
-        nc.sync.dma_start(out=bias_row[0:1, PACK, :], in_=biases[C:J].unsqueeze(0))
+
+        def load_bias():
+            nc.sync.dma_start(
+                out=bias_row[0:1, 0:PACK, :],
+                in_=biases[0:C].unsqueeze(0).unsqueeze(0).to_broadcast([1, PACK, C]),
+            )
+            nc.sync.dma_start(out=bias_row[0:1, PACK, :], in_=biases[C:J].unsqueeze(0))
+
         load_s(0)
         load_x(0)
         load_s(1)
+        load_bias()
         load_s(2)
         load_s(3)
-        load_x(1)
         load_w(2)
         load_w(1)
+        load_x(1)
         load_w(0)
         load_x(2)
         load_x(3)
@@ -278,44 +283,113 @@ def tile_conv_st_pa_t_kernel(tc, inputs, supports, weights, biases, out):
             nc.scalar.copy(out=bias_f[:], in_=bank[:, 0, :])
 
         regroup_s(0)
+        quantise_s(0)
         regroup_x(0)
         regroup_s(1)
-        quantise_s(0)
-        quantise_x(0)
-        regroup_s(2)
-        quantise_s(1)
         spread_bias()
-        add_bias_to_x(0)
+        quantise_x(0)
+        quantise_s(1)
+        regroup_s(2)
         add_bias_to_x(1)
+        quantise_s(2, (1,))
+        quantise_s(2, (3,))
         regroup_s(3)
-        for ch in range(NCH):
-            quantise_s(2, (ch,))
-            quantise_s(3, (ch,))
+        quantise_s(2, (2,))
+        quantise_s(2, (0,))
+        quantise_s(3, (0,))
+        quantise_s(3, (1,))
+        add_bias_to_x(0)
+        quantise_s(3, (2,))
+        quantise_s(3, (3,))
+        regroup_w(2)
         stage1(0)
         stage1(1)
         regroup_x(1)
-        regroup_w(2)
+        regroup_w(1)
+        add_bias_to_x(2)
         quantise_x(1)
         quantise_w(2)
-        quantise_z(0)
-        add_bias_to_x(2)
-        add_bias_to_x(3)
-        regroup_w(1)
         regroup_w(0)
+        quantise_z(0)
         quantise_w(1)
+        stage1(2)
+        regroup_x(2)
+        stage2(0)
+        stage1(3)
+        quantise_z(1)
+        quantise_x(2)
         quantise_w(0)
-        for s in range(BT + 1):
-            if s + LEAD < BT:
-                stage1(s + LEAD)
-            if s + 1 < BT:
-                quantise_z(s + 1)
-            if s >= 1:
-                finish(s - 1)
-            if s < BT:
-                stage2(s)
-            if 4 <= s + 2 < BT:
-                add_bias_to_x(s + 2)
-            if s in RG_AT:
-                regroup_x(RG_AT[s])
-            if s in Q_AT:
-                quantise_x(Q_AT[s])
+        quantise_z(2)
+        finish(0)
+        stage2(1)
+        regroup_x(3)
+        stage1(4)
+        quantise_z(3)
+        finish(1)
+        stage2(2)
+        stage1(5)
+        quantise_z(4)
+        add_bias_to_x(3)
+        finish(2)
+        stage2(3)
+        add_bias_to_x(5)
+        stage1(6)
+        add_bias_to_x(4)
+        quantise_z(5)
+        finish(3)
+        stage2(4)
+        quantise_x(3)
+        stage1(7)
+        quantise_z(6)
+        finish(4)
+        stage2(5)
+        add_bias_to_x(7)
+        stage1(8)
+        quantise_z(7)
+        add_bias_to_x(6)
+        finish(5)
+        stage2(6)
+        regroup_x(4)
+        stage1(9)
+        quantise_z(8)
+        finish(6)
+        stage2(7)
+        add_bias_to_x(9)
+        stage1(10)
+        add_bias_to_x(8)
+        finish(7)
+        stage2(8)
+        quantise_z(9)
+        quantise_x(4)
+        stage1(11)
+        quantise_z(10)
+        finish(8)
+        stage2(9)
+        add_bias_to_x(10)
+        stage1(12)
+        quantise_z(11)
+        finish(9)
+        stage2(10)
+        add_bias_to_x(12)
+        add_bias_to_x(11)
+        stage1(13)
+        quantise_z(12)
+        finish(10)
+        stage2(11)
+        add_bias_to_x(15)
+        add_bias_to_x(13)
+        stage1(14)
+        quantise_z(13)
+        finish(11)
+        stage2(12)
+        add_bias_to_x(14)
+        stage1(15)
+        quantise_z(14)
+        finish(12)
+        stage2(13)
+        quantise_z(15)
+        finish(13)
+        stage2(14)
+        finish(14)
+        stage2(15)
+        finish(15)

@@ -31,10 +31,13 @@ FINE = {15: 2}
 FLOPS = 2 * BT * C * ORDER * N * N + 2 * B * (1 + 2 + 3 * (T - 2)) * N * C * ORDER * J
 
 
-def by_fours(dst, src):
+RUN = 8
+
+
+def by_runs(dst, src):
     return (
-        dst.rearrange("p (c i) t -> p c t i", i=4),
-        src.rearrange("p t (c i) -> p c t i", i=4),
+        dst.rearrange("p (c i) t -> p c t i", i=RUN),
+        src.rearrange("p t (c i) -> p c t i", i=RUN),
     )
 
 
@@ -120,12 +123,12 @@ def tile_conv_st_pa_t_kernel(tc, inputs, supports, weights, biases, out):
             grp_x[g] = stage.tile([P, hi - lo, C, PACK], BF16, name="grp_x%d" % g, tag="grp_x", align_bytes=64)
             if g in (0,):
                 for s in range(hi - lo):
-                    d, r = by_fours(grp_x[g][:, s], raw_x[:, lo + s])
+                    d, r = by_runs(grp_x[g][:, s], raw_x[:, lo + s])
                     nc.scalar.copy(out=d, in_=r)
             else:
                 nc.vector.tensor_copy(
-                    out=grp_x[g][:].rearrange("p s (c i) t -> p s c t i", i=4),
-                    in_=raw_x[:, lo:hi].rearrange("p s t (c i) -> p s c t i", i=4),
+                    out=grp_x[g][:].rearrange("p s (c i) t -> p s c t i", i=RUN),
+                    in_=raw_x[:, lo:hi].rearrange("p s t (c i) -> p s c t i", i=RUN),
                 )
 
         def quantise_x(g):
@@ -141,9 +144,9 @@ def tile_conv_st_pa_t_kernel(tc, inputs, supports, weights, biases, out):
         def regroup_s(o):
             cut = S_SPLITS[o]
             grp_s[o] = stage.tile([P, N, PACK], BF16, name="grp_s%d" % o, tag="grp_s", bufs=3, align_bytes=64)
-            d, r = by_fours(grp_s[o][:, 0:cut], raw_s[o][:, :, 0:cut])
+            d, r = by_runs(grp_s[o][:, 0:cut], raw_s[o][:, :, 0:cut])
             nc.vector.tensor_copy(out=d, in_=r)
-            d, r = by_fours(grp_s[o][:, cut:N], raw_s[o][:, :, cut:N])
+            d, r = by_runs(grp_s[o][:, cut:N], raw_s[o][:, :, cut:N])
             nc.scalar.copy(out=d, in_=r)
 
         def quantise_s(o, chunks=(0, 1, 2, 3)):
@@ -155,7 +158,7 @@ def tile_conv_st_pa_t_kernel(tc, inputs, supports, weights, biases, out):
                 )
 
         def regroup_w(k):
-            d, r = by_fours(grp_w[:, k], raw_w[:, k])
+            d, r = by_runs(grp_w[:, k], raw_w[:, k])
             nc.vector.tensor_copy(out=d, in_=r)
 
         def quantise_w(k):

@@ -18,14 +18,10 @@ PACK = 4
 BT = B * T
 J = 2 * C
 NCH = N // P
-LEAD = 2
 X_GROUPS = [(0, 2), (2, 4), (4, 8), (8, 12), (12, 16)]
 S_SPLITS = [288, 288, 288, 320]
 XB_PE = (0, 1)
 XB_G = ()
-EVAC_V = ()
-RG_AT = {0: 2, 3: 3, 7: 4}
-Q_AT = {1: 2, 4: 3, 8: 4}
 FINE = {15: 2}
 
 FLOPS = 2 * BT * C * ORDER * N * N + 2 * B * (1 + 2 + 3 * (T - 2)) * N * C * ORDER * J
@@ -189,6 +185,13 @@ def tile_conv_st_pa_t_kernel(tc, inputs, supports, weights, biases, out):
                     op=ADD,
                 )
 
+        waiting = []
+
+        def sigmoid_waiting():
+            while waiting:
+                bt = waiting.pop(0)
+                nc.scalar.activation(out=sig[bt][:], in_=gate[bt][:], func=SIGMOID)
+
         z_bf = {}
 
         def stage1(bt):
@@ -207,10 +210,9 @@ def tile_conv_st_pa_t_kernel(tc, inputs, supports, weights, biases, out):
                 )
                 dst = zt[:, :, ch * 32 : (ch + 1) * 32, :]
                 src = bank[:].rearrange("p (o l q) -> p q l o", o=ORDER, q=PACK)
-                if (bt, ch) in EVAC_V:
-                    nc.vector.tensor_copy(out=dst, in_=src)
-                else:
-                    nc.scalar.copy(out=dst, in_=src)
+                nc.scalar.copy(out=dst, in_=src)
+                if ch == 0:
+                    sigmoid_waiting()
 
         def quantise_z(bt):
             nc.vector.quantize_mx(
@@ -264,9 +266,11 @@ def tile_conv_st_pa_t_kernel(tc, inputs, supports, weights, biases, out):
                         op=ADD,
                     )
             if width > 2:
-                nc.scalar.activation(out=sig[bt][:], in_=gate[bt][:], func=SIGMOID)
+                waiting.append(bt)
 
         def finish(bt):
+            if bt in waiting:
+                sigmoid_waiting()
             res = epi.tile([P, PACK, C], F32, name="res%d" % bt, tag="res")
             width = FINE.get(bt, PACK)
             eng = nc.gpsimd if bt not in FINE else nc.vector

from contextlib import ExitStack

import concourse.mybir as mybir
from concourse.masks import make_identity

BF16 = mybir.dt.bfloat16
F32 = mybir.dt.float32
U32 = mybir.dt.uint32
U8 = mybir.dt.uint8
FP8X4 = mybir.dt.float8_e4m3fn_x4
ADD = mybir.AluOpType.add
MULT = mybir.AluOpType.mult
SIGMOID = mybir.ActivationFunctionType.Sigmoid

B, T, N, C, ORDER, KT = 2, 8, 512, 128, 4, 3
P = 128
PACK = 4
BT = B * T
J = 2 * C
NCH = N // P
X_GROUPS = [(0, 2), (2, 4), (4, 8), (8, 12), (12, 16)]
S_SPLITS = [288, 288, 288, 320]
XB_PE = (0, 1)
XB_G = ()
FINE = {15: 2}

FLOPS = 2 * BT * C * ORDER * N * N + 2 * B * (1 + 2 + 3 * (T - 2)) * N * C * ORDER * J


RUN = 8


def by_runs(dst, src):
    return (
        dst.rearrange("p (c i) t -> p c t i", i=RUN),
        src.rearrange("p t (c i) -> p c t i", i=RUN),
    )


def tile_conv_st_pa_t_kernel(tc, inputs, supports, weights, biases, out):
    nc = tc.nc
    x_dram = inputs.rearrange("b t (p j) c -> p (b t) (j c)", j=PACK)
    s_dram = supports.rearrange("(p j) (o n) -> p o j n", j=PACK, o=ORDER)
    w_dram = weights.rearrange("(k p t) j -> p k (t j)", k=KT, t=PACK)
    out_dram = out.rearrange("b t (p q) c -> p (b t) (q c)", q=PACK)

    with ExitStack() as ctx:
        keep = ctx.enter_context(tc.tile_pool(name="keep", bufs=1))
        stage = ctx.enter_context(tc.tile_pool(name="stage", bufs=2))
        epi = ctx.enter_context(tc.tile_pool(name="epi", bufs=3))
        psum = ctx.enter_context(tc.psum_pool(name="psum", bufs=1))
        ctx.enter_context(tc.manual_schedule())

        raw_x = keep.tile([P, BT, PACK, C], BF16, name="raw_x")
        x_codes = keep.tile([P, BT, C], U32, name="x_codes", align_bytes=64)
        x_scales = keep.tile([P, BT, C], U8, name="x_scales", align_bytes=64)
        s_codes = keep.tile([P, NCH, ORDER, P], U32, name="s_codes", align_bytes=64)
        s_scales = keep.tile([P, NCH, ORDER, P], U8, name="s_scales", align_bytes=64)
        raw_w = keep.tile([P, KT, PACK, J], BF16, name="raw_w")
        grp_w = keep.tile([P, KT, J, PACK], BF16, name="grp_w", align_bytes=64)
        w_codes = keep.tile([P, KT, J], U32, name="w_codes", align_bytes=64)
        w_scales = keep.tile([P, KT, J], U8, name="w_scales", align_bytes=64)
        z_codes = keep.tile([P, BT, N], U32, name="z_codes", align_bytes=64)
        z_scales = keep.tile([P, BT, N], U8, name="z_scales", align_bytes=64)
        bias_row = keep.tile([P, PACK + 1, C], BF16, name="bias_row")
        ident = keep.tile([P, P], BF16, name="ident")
        ones = keep.tile([P, P], BF16, name="ones")
        bias_f = keep.tile([P, J], F32, name="bias_f")
        xb = keep.tile([P, BT, PACK, C], F32, name="xb")
        warm_in = keep.tile([P, 1], F32, name="warm_in")
        warm_out = keep.tile([P, 1], F32, name="warm_out")

        def load_x(g):
            lo, hi = X_GROUPS[g]
            nc.sync.dma_start(
                out=raw_x[:, lo:hi].rearrange("p s j c -> p s (j c)"), in_=x_dram[:, lo:hi, :]
            )

        raw_s = {}

        def load_s(o):
            raw_s[o] = stage.tile([P, PACK, N], BF16, name="raw_s%d" % o, tag="raw_s", bufs=ORDER)
            nc.sync.dma_start(out=raw_s[o][:], in_=s_dram[:, o])

        def load_w(k):
            nc.sync.dma_start(out=raw_w[:, k].rearrange("p t j -> p (t j)"), in_=w_dram[:, k, :])

        nc.vector.memset(warm_in[:], 0.0)
        nc.vector.memset(bias_row[:], 0.0)
        nc.vector.memset(ones[:], 1.0)
        make_identity(nc, ident[:])

        def load_bias():
            nc.sync.dma_start(
                out=bias_row[0:1, 0:PACK, :],
                in_=biases[0:C].unsqueeze(0).unsqueeze(0).to_broadcast([1, PACK, C]),
            )
            nc.sync.dma_start(out=bias_row[0:1, PACK, :], in_=biases[C:J].unsqueeze(0))

        load_s(0)
        load_x(0)
        load_s(1)
        load_bias()
        load_s(2)
        load_s(3)
        load_w(2)
        load_w(1)
        load_x(1)
        load_w(0)
        load_x(2)
        load_x(3)
        load_x(4)
        nc.scalar.activation(out=warm_out[:], in_=warm_in[:], func=SIGMOID)

        grp_x = {}

        def regroup_x(g):
            lo, hi = X_GROUPS[g]
            grp_x[g] = stage.tile([P, hi - lo, C, PACK], BF16, name="grp_x%d" % g, tag="grp_x", align_bytes=64)
            if g in (0,):
                for s in range(hi - lo):
                    d, r = by_runs(grp_x[g][:, s], raw_x[:, lo + s])
                    nc.scalar.copy(out=d, in_=r)
            else:
                nc.vector.tensor_copy(
                    out=grp_x[g][:].rearrange("p s (c i) t -> p s c t i", i=RUN),
                    in_=raw_x[:, lo:hi].rearrange("p s t (c i) -> p s c t i", i=RUN),
                )

        def quantise_x(g):
            lo, hi = X_GROUPS[g]
            nc.vector.quantize_mx(
                out=x_codes[:, lo:hi].rearrange("p s c -> p (s c)").bitcast(FP8X4),
                scales=x_scales[:, lo:hi].rearrange("p s c -> p (s c)"),
                in_=grp_x[g][:].rearrange("p s c t -> p (s c t)"),
            )

        grp_s = {}

        def regroup_s(o):
            cut = S_SPLITS[o]
            grp_s[o] = stage.tile([P, N, PACK], BF16, name="grp_s%d" % o, tag="grp_s", bufs=3, align_bytes=64)
            d, r = by_runs(grp_s[o][:, 0:cut], raw_s[o][:, :, 0:cut])
            nc.vector.tensor_copy(out=d, in_=r)
            d, r = by_runs(grp_s[o][:, cut:N], raw_s[o][:, :, cut:N])
            nc.scalar.copy(out=d, in_=r)

        def quantise_s(o, chunks=(0, 1, 2, 3)):
            for ch in chunks:
                nc.vector.quantize_mx(
                    out=s_codes[:, ch, o, :].bitcast(FP8X4),
                    scales=s_scales[:, ch, o, :],
                    in_=grp_s[o][:, ch * P : (ch + 1) * P, :].rearrange("p w t -> p (w t)"),
                )

        def regroup_w(k):
            d, r = by_runs(grp_w[:, k], raw_w[:, k])
            nc.vector.tensor_copy(out=d, in_=r)

        def quantise_w(k):
            nc.vector.quantize_mx(
                out=w_codes[:, k, :].bitcast(FP8X4),
                scales=w_scales[:, k, :],
                in_=grp_w[:, k].rearrange("p j t -> p (j t)"),
            )

        def add_bias_to_x(bt):
            if bt in XB_PE:
                bank = psum.tile([P, N], F32, name="xb_%d" % bt, tag="s1", bufs=5)
                nc.tensor.matmul(
                    out=bank[:], lhsT=ident[:], rhs=raw_x[:, bt].rearrange("p j c -> p (j c)"),
                    start=True, stop=False,
                )
                nc.tensor.matmul(
                    out=bank[:], lhsT=ones[:], rhs=bias_row[:, 0:PACK].rearrange("p r c -> p (r c)"),
                    start=False, stop=True,
                )
                nc.scalar.copy(out=xb[:, bt].rearrange("p j c -> p (j c)"), in_=bank[:])
            else:
                eng = nc.gpsimd if bt in XB_G else nc.vector
                eng.tensor_tensor(
                    out=xb[:, bt],
                    in0=raw_x[:, bt],
                    in1=bias_f[:, 0:C].unsqueeze(1).to_broadcast([P, PACK, C]),
                    op=ADD,
                )

        waiting = []

        def sigmoid_waiting():
            while waiting:
                bt = waiting.pop(0)
                nc.scalar.activation(out=sig[bt][:], in_=gate[bt][:], func=SIGMOID)

        z_bf = {}

        def stage1(bt):
            zt = stage.tile([P, PACK, P, ORDER], BF16, name="z_bf%d" % bt, tag="z_bf", bufs=3, align_bytes=64)
            z_bf[bt] = zt
            for ch in range(NCH):
                bank = psum.tile([P, N], F32, name="s1_%d_%d" % (bt, ch), tag="s1", bufs=5)
                nc.tensor.matmul_mx(
                    out=bank[:],
                    lhsT=x_codes[:, bt, :].bitcast(FP8X4),
                    lhsT_scale=x_scales[:, bt, :],
                    rhs=s_codes[:, ch].rearrange("p o n -> p (o n)").bitcast(FP8X4),
                    rhs_scale=s_scales[:, ch].rearrange("p o n -> p (o n)"),
                    start=True,
                    stop=True,
                )
                dst = zt[:, :, ch * 32 : (ch + 1) * 32, :]
                src = bank[:].rearrange("p (o l q) -> p q l o", o=ORDER, q=PACK)
                nc.scalar.copy(out=dst, in_=src)
                if ch == 0:
                    sigmoid_waiting()

        def quantise_z(bt):
            nc.vector.quantize_mx(
                out=z_codes[:, bt, :].bitcast(FP8X4),
                scales=z_scales[:, bt, :],
                in_=z_bf[bt][:].rearrange("p q n o -> p (q n o)"),
            )

        val = {}
        gate = {}
        sig = {}

        def stage2(bt):
            t = bt % T
            taps = [(k, bt - (KT - 1 - k)) for k in range(KT) if t - (KT - 1 - k) >= 0]
            val[bt] = epi.tile([P, PACK, C], F32, name="val%d" % bt, tag="val")
            gate[bt] = epi.tile([P, PACK, C], F32, name="gate%d" % bt, tag="gate")
            sig[bt] = epi.tile([P, PACK, C], F32, name="sig%d" % bt, tag="sig")
            width = FINE.get(bt, PACK)
            for h in range(2):
                bank = psum.tile([P, 2, J], F32, name="s2_%d_%d" % (bt, h), tag="s2", bufs=3)
                for qq in range(2):
                    q = 2 * h + qq
                    for n_done, (k, src) in enumerate(taps):
                        nc.tensor.matmul_mx(
                            out=bank[:, qq, :],
                            lhsT=z_codes[:, src, q * P : (q + 1) * P].bitcast(FP8X4),
                            lhsT_scale=z_scales[:, src, q * P : (q + 1) * P],
                            rhs=w_codes[:, k, :].bitcast(FP8X4),
                            rhs_scale=w_scales[:, k, :],
                            start=(n_done == 0),
                            stop=(n_done == len(taps) - 1),
                        )
                step = min(width, 2)
                for a in range(0, 2, step):
                    lo = 2 * h + a
                    nc.vector.tensor_tensor(
                        out=gate[bt][:, lo : lo + step, :],
                        in0=bank[:, a : a + step, C:J],
                        in1=bias_f[:, C:J].unsqueeze(1).to_broadcast([P, step, C]),
                        op=ADD,
                    )
                    if width <= 2:
                        nc.scalar.activation(
                            out=sig[bt][:, lo : lo + step, :], in_=gate[bt][:, lo : lo + step, :], func=SIGMOID
                        )
                    nc.vector.tensor_tensor(
                        out=val[bt][:, lo : lo + step, :],
                        in0=bank[:, a : a + step, 0:C],
                        in1=xb[:, bt, lo : lo + step, :],
                        op=ADD,
                    )
            if width > 2:
                waiting.append(bt)

        def finish(bt):
            if bt in waiting:
                sigmoid_waiting()
            res = epi.tile([P, PACK, C], F32, name="res%d" % bt, tag="res")
            width = FINE.get(bt, PACK)
            eng = nc.gpsimd if bt not in FINE else nc.vector
            for lo in range(0, PACK, width):
                hi = lo + width
                eng.tensor_tensor(out=res[:, lo:hi], in0=val[bt][:, lo:hi], in1=sig[bt][:, lo:hi], op=MULT)
                nc.sync.dma_start(
                    out=out_dram[:, bt, lo * C : hi * C], in_=res[:, lo:hi].rearrange("p q c -> p (q c)")
                )

        def spread_bias():
            bank = psum.tile([P, 2, J], F32, name="bias_bank", tag="s2", bufs=3)
            nc.tensor.matmul(
                out=bank[:, 0, :], lhsT=ones[:], rhs=bias_row[:, PACK - 1 : PACK + 1].rearrange("p r c -> p (r c)"),
                start=True, stop=True,
            )
            nc.scalar.copy(out=bias_f[:], in_=bank[:, 0, :])

        regroup_s(0)
        quantise_s(0)
        regroup_x(0)
        regroup_s(1)
        spread_bias()
        quantise_x(0)
        quantise_s(1)
        regroup_s(2)
        add_bias_to_x(1)
        quantise_s(2, (1,))
        quantise_s(2, (3,))
        regroup_s(3)
        quantise_s(2, (2,))
        quantise_s(2, (0,))
        quantise_s(3, (0,))
        quantise_s(3, (1,))
        add_bias_to_x(0)
        quantise_s(3, (2,))
        quantise_s(3, (3,))
        regroup_w(2)
        stage1(0)
        stage1(1)
        regroup_x(1)
        regroup_w(1)
        add_bias_to_x(2)
        quantise_x(1)
        quantise_w(2)
        regroup_w(0)
        quantise_z(0)
        quantise_w(1)
        stage1(2)
        regroup_x(2)
        stage2(0)
        stage1(3)
        quantise_z(1)
        quantise_x(2)
        quantise_w(0)
        quantise_z(2)
        finish(0)
        stage2(1)
        regroup_x(3)
        stage1(4)
        quantise_z(3)
        finish(1)
        stage2(2)
        stage1(5)
        quantise_z(4)
        add_bias_to_x(3)
        finish(2)
        stage2(3)
        add_bias_to_x(5)
        stage1(6)
        add_bias_to_x(4)
        quantise_z(5)
        finish(3)
        stage2(4)
        quantise_x(3)
        stage1(7)
        quantise_z(6)
        finish(4)
        stage2(5)
        add_bias_to_x(7)
        stage1(8)
        quantise_z(7)
        add_bias_to_x(6)
        finish(5)
        stage2(6)
        regroup_x(4)
        stage1(9)
        quantise_z(8)
        finish(6)
        stage2(7)
        add_bias_to_x(9)
        stage1(10)
        add_bias_to_x(8)
        finish(7)
        stage2(8)
        quantise_z(9)
        quantise_x(4)
        stage1(11)
        quantise_z(10)
        finish(8)
        stage2(9)
        add_bias_to_x(10)
        stage1(12)
        quantise_z(11)
        finish(9)
        stage2(10)
        add_bias_to_x(12)
        add_bias_to_x(11)
        stage1(13)
        quantise_z(12)
        finish(10)
        stage2(11)
        add_bias_to_x(15)
        add_bias_to_x(13)
        stage1(14)
        quantise_z(13)
        finish(11)
        stage2(12)
        add_bias_to_x(14)
        stage1(15)
        quantise_z(14)
        finish(12)
        stage2(13)
        quantise_z(15)
        finish(13)
        stage2(14)
        finish(14)
        stage2(15)
        finish(15)
